import numpy as np
import ml_dtypes


def mxq(x, axis, fmt="e4m3"):
    dtype, down = {"e4m3": (ml_dtypes.float8_e4m3fn, 7), "e5m2": (ml_dtypes.float8_e5m2, 14)}[fmt]
    v = np.moveaxis(np.asarray(x, np.float32).astype(ml_dtypes.bfloat16).astype(np.float64), axis, -1)
    blocks = v.reshape(v.shape[:-1] + (-1, 32))
    amax = np.abs(blocks).max(-1, keepdims=True)
    byte = np.maximum(np.where(amax > 0, np.frexp(amax)[1] - 1 + 127, 0) - down, 1)
    scale = np.exp2(byte - 127.0)
    codes = (blocks / scale).astype(np.float32).astype(dtype).astype(np.float64)
    return np.moveaxis((codes * scale).reshape(v.shape), -1, axis)


WIDE = False


def mx_kscale(k):
    if not WIDE:
        return np.ones(k)
    levels = np.array([20, -20, 10, -10, 0])
    a = np.random.permutation(np.resize(levels, k // 512 * 4)).reshape(k // 512, 4)
    idx = np.arange(k)
    return np.exp2(a[idx // 512, idx % 128 // 32])


BF16 = ml_dtypes.bfloat16


def bf(x):
    return np.asarray(x, np.float32).astype(BF16)


def f64(x):
    return np.asarray(x).astype(np.float64)


B, N, K, D, L = 2, 1024, 7, 512, 1024


def degree(a):
    factor = f64(a).sum(axis=-1, keepdims=True)
    return np.where(factor > 0.5, factor, np.ones_like(factor))


def setup_inputs():
    u = mx_kscale(L)
    limit = np.sqrt(6.0 / (D + L))
    lone = np.random.random((B, N, 1)) < 0.125
    a = bf((0.3 + 0.7 * np.random.random((B, N, K + 1))) * np.where(lone, 0.4 / (K + 1), 1.0))
    targets = bf(np.random.standard_normal((B, N, D)))
    neighbors = bf(np.random.standard_normal((B, N, K, D)))
    kernel0 = bf(np.random.uniform(-limit, limit, (D, L)))
    g = bf(np.random.standard_normal((B, N, L)) * np.exp2(np.random.randint(-12, 1, (B, N, 1))) * 32.0 * u)
    z = ((f64(targets) + f64(neighbors).sum(axis=-2)) @ f64(kernel0)) / degree(a)
    return {"targets": targets, "neighbors": neighbors, "a": a,
            "kernel": bf(f64(kernel0) / u[None, :]),
            "z": np.asarray(z, np.float32), "grad_out": g}


def reference(targets, neighbors, a, kernel, z, grad_out):
    factor = degree(a)
    dz = f64(grad_out) * np.where(f64(z) > 0.0, 1.0, 0.0) / factor
    return mxq(dz, 2, "e5m2") @ mxq(f64(kernel), 1, "e4m3").T

@@ -1,0 +1,146 @@
+from contextlib import ExitStack
+
+import concourse.mybir as mybir
+from concourse.masks import make_identity
+
+F32 = mybir.dt.float32
+BF16 = mybir.dt.bfloat16
+U32 = mybir.dt.uint32
+U8 = mybir.dt.uint8
+E4M3_X4 = mybir.dt.float8_e4m3fn_x4
+E5M2_X4 = mybir.dt.float8_e5m2_x4
+ALU = mybir.AluOpType
+
+P = 128
+PACK = 4
+PAIR = 2
+HALVES = PACK // PAIR
+
+NODES = 2 * 1024
+NEIGHBOURS = 8
+L = 1024
+D = 512
+
+PASSES = L // (P * PACK)
+ROW_TILES = NODES // P
+KERNEL_TILES = D // P
+TILES_PER_LOAD = 2
+TILES_PER_STORE = 2
+LOADS = ROW_TILES // TILES_PER_LOAD
+STORES = ROW_TILES // TILES_PER_STORE
+
+FLOPS = 2 * NODES * L * D
+BYTES = NODES * NEIGHBOURS * 2 + D * L * 2 + NODES * L * 4 + NODES * L * 2 + NODES * D * 4
+
+
+def turn_rows(nc, banks, identity, rows, grouped):
+    words = rows.bitcast(F32)
+    turned = banks.tile([P, PASSES * HALVES, P], F32)
+    for i in range(PASSES * HALVES):
+        nc.tensor.transpose(turned[:, i, :], words[:, i * P : (i + 1) * P], identity)
+    nc.scalar.copy(out=grouped, in_=turned[:].rearrange("p (g u) r -> p g r u", u=HALVES))
+
+
+def tile_singlegcnlayer_t_v_kernel(tc, targets, neighbors, a, kernel, z, grad_out, out):
+    nc = tc.nc
+
+    a_rows = a.flatten_outer_dims().rearrange("(p t) k -> p t k", t=ROW_TILES)
+    z_rows = z.flatten_outer_dims().rearrange("(p t) l -> p t l", t=ROW_TILES)
+    g_rows = grad_out.flatten_outer_dims().rearrange("(p t) l -> p t l", t=ROW_TILES)
+    out_rows = out.flatten_outer_dims().rearrange("(p t) d -> p t d", t=ROW_TILES)
+    kernel_rows = kernel.rearrange("(j p) l -> p j l", p=P)
+
+    with ExitStack() as ctx:
+        keep = ctx.enter_context(tc.tile_pool(name="keep", bufs=1))
+        stream = ctx.enter_context(tc.tile_pool(name="stream", bufs=LOADS))
+        results = ctx.enter_context(tc.tile_pool(name="results", bufs=STORES))
+        work = ctx.enter_context(tc.tile_pool(name="work", bufs=4))
+        banks = ctx.enter_context(tc.psum_pool(name="banks", bufs=4))
+        sums = ctx.enter_context(tc.psum_pool(name="sums", bufs=4))
+
+        a_sb = keep.tile([P, ROW_TILES, NEIGHBOURS], BF16)
+        nc.sync.dma_start(out=a_sb[:], in_=a_rows)
+        kernel_sb = keep.tile([P, KERNEL_TILES, L], BF16)
+        g_loaded = []
+        z_loaded = []
+        for c in range(LOADS):
+            tiles = slice(c * TILES_PER_LOAD, (c + 1) * TILES_PER_LOAD)
+            g_sb = stream.tile([P, TILES_PER_LOAD, L], BF16)
+            nc.sync.dma_start(out=g_sb[:], in_=g_rows[:, tiles, :])
+            g_loaded.append(g_sb)
+            z_sb = stream.tile([P, TILES_PER_LOAD, L], F32)
+            nc.sync.dma_start(out=z_sb[:], in_=z_rows[:, tiles, :])
+            z_loaded.append(z_sb)
+            if c == 0:
+                nc.sync.dma_start(out=kernel_sb[:], in_=kernel_rows)
+
+        identity = keep.tile([P, P], F32)
+        make_identity(nc, identity[:])
+
+        degree = keep.tile([P, ROW_TILES], F32)
+        nc.vector.tensor_reduce(out=degree[:], in_=a_sb[:], axis=mybir.AxisListType.X, op=ALU.add)
+        factor = keep.tile([P, ROW_TILES], F32)
+        nc.vector.scalar_tensor_tensor(
+            out=factor[:], in0=degree[:], scalar=0.5, in1=degree[:], op0=ALU.is_le, op1=ALU.max
+        )
+        inv_factor = keep.tile([P, ROW_TILES], F32)
+        nc.vector.reciprocal(out=inv_factor[:], in_=factor[:])
+
+        kernel_grouped = keep.tile([P, PASSES * D * PACK], BF16, align_bytes=64)
+        kernel_words = kernel_grouped[:].bitcast(F32).rearrange(
+            "p (g d u) -> p g d u", g=PASSES, u=HALVES
+        )
+        for j in range(KERNEL_TILES):
+            turn_rows(nc, banks, identity[:], kernel_sb[:, j, :], kernel_words[:, :, j * P : (j + 1) * P, :])
+        kernel_codes = keep.tile([P, PASSES * D], U32, align_bytes=64)
+        kernel_scales = keep.tile([P, PASSES * D], U8, align_bytes=64)
+        nc.vector.quantize_mx(
+            out=kernel_codes[:].bitcast(E4M3_X4), scales=kernel_scales[:], in_=kernel_grouped[:]
+        )
+
+        dz_codes = keep.tile([P, ROW_TILES, PASSES * P], U32, align_bytes=64)
+        dz_scales = keep.tile([P, ROW_TILES, PASSES * P], U8, align_bytes=64)
+        for s in range(STORES):
+            out_sb = results.tile([P, TILES_PER_STORE, D], F32)
+            for i in range(TILES_PER_STORE):
+                t = s * TILES_PER_STORE + i
+                g_tile = g_loaded[t // TILES_PER_LOAD][:, t % TILES_PER_LOAD, :]
+                z_tile = z_loaded[t // TILES_PER_LOAD][:, t % TILES_PER_LOAD, :]
+
+                masked = work.tile([P, L], BF16)
+                nc.vector.scalar_tensor_tensor(
+                    out=masked[:], in0=z_tile, scalar=0.0, in1=g_tile, op0=ALU.is_gt, op1=ALU.mult
+                )
+                dz = work.tile([P, L], BF16)
+                nc.vector.tensor_scalar(
+                    out=dz[:], in0=masked[:], scalar1=inv_factor[:, t : t + 1], scalar2=None, op0=ALU.mult
+                )
+
+                grouped = work.tile([P, PASSES * P * PACK], BF16, align_bytes=64)
+                turn_rows(
+                    nc,
+                    banks,
+                    identity[:],
+                    dz[:],
+                    grouped[:].bitcast(F32).rearrange("p (g r u) -> p g r u", g=PASSES, u=HALVES),
+                )
+                nc.vector.quantize_mx(
+                    out=dz_codes[:, t, :].bitcast(E5M2_X4), scales=dz_scales[:, t, :], in_=grouped[:]
+                )
+
+                acc = sums.tile([P, D], F32)
+                for g in range(PASSES):
+                    nodes = slice(g * P, (g + 1) * P)
+                    columns = slice(g * D, (g + 1) * D)
+                    nc.tensor.matmul_mx(
+                        out=acc[:],
+                        lhsT=dz_codes[:, t, nodes].bitcast(E5M2_X4),
+                        lhsT_scale=dz_scales[:, t, nodes],
+                        rhs=kernel_codes[:, columns].bitcast(E4M3_X4),
+                        rhs_scale=kernel_scales[:, columns],
+                        start=(g == 0),
+                        stop=(g == PASSES - 1),
+                    )
+                nc.scalar.copy(out=out_sb[:, i, :], in_=acc[:])
+            tiles = slice(s * TILES_PER_STORE, (s + 1) * TILES_PER_STORE)
+            nc.sync.dma_start(out=out_rows[:, tiles, :], in_=out_sb[:])

@@ -24,10 +24,11 @@ D = 512
 PASSES = L // (P * PACK)
 ROW_TILES = NODES // P
 KERNEL_TILES = D // P
-TILES_PER_LOAD = 2
+TILES_PER_LOAD = 1
 TILES_PER_STORE = 2
 LOADS = ROW_TILES // TILES_PER_LOAD
 STORES = ROW_TILES // TILES_PER_STORE
+LAG = 2
 
 FLOPS = 2 * NODES * L * D
 BYTES = NODES * NEIGHBOURS * 2 + D * L * 2 + NODES * L * 4 + NODES * L * 2 + NODES * D * 4
@@ -51,16 +52,18 @@ def tile_singlegcnlayer_t_v_kernel(tc, targets, neighbors, a, kernel, z, grad_ou
     kernel_rows = kernel.rearrange("(j p) l -> p j l", p=P)
 
     with ExitStack() as ctx:
+        ctx.enter_context(tc.manual_schedule())
         keep = ctx.enter_context(tc.tile_pool(name="keep", bufs=1))
         stream = ctx.enter_context(tc.tile_pool(name="stream", bufs=LOADS))
         results = ctx.enter_context(tc.tile_pool(name="results", bufs=STORES))
-        work = ctx.enter_context(tc.tile_pool(name="work", bufs=4))
+        work = ctx.enter_context(tc.tile_pool(name="work", bufs=LAG + 2))
         banks = ctx.enter_context(tc.psum_pool(name="banks", bufs=4))
         sums = ctx.enter_context(tc.psum_pool(name="sums", bufs=4))
 
         a_sb = keep.tile([P, ROW_TILES, NEIGHBOURS], BF16)
         nc.sync.dma_start(out=a_sb[:], in_=a_rows)
         kernel_sb = keep.tile([P, KERNEL_TILES, L], BF16)
+        nc.sync.dma_start(out=kernel_sb[:], in_=kernel_rows)
         g_loaded = []
         z_loaded = []
         for c in range(LOADS):
@@ -71,8 +74,10 @@ def tile_singlegcnlayer_t_v_kernel(tc, targets, neighbors, a, kernel, z, grad_ou
             z_sb = stream.tile([P, TILES_PER_LOAD, L], F32)
             nc.sync.dma_start(out=z_sb[:], in_=z_rows[:, tiles, :])
             z_loaded.append(z_sb)
-            if c == 0:
-                nc.sync.dma_start(out=kernel_sb[:], in_=kernel_rows)
+        out_stored = []
+        for s in range(STORES):
+            out_sb = results.tile([P, TILES_PER_STORE, D], F32)
+            out_stored.append(out_sb)
 
         identity = keep.tile([P, P], F32)
         make_identity(nc, identity[:])
@@ -94,53 +99,62 @@ def tile_singlegcnlayer_t_v_kernel(tc, targets, neighbors, a, kernel, z, grad_ou
             turn_rows(nc, banks, identity[:], kernel_sb[:, j, :], kernel_words[:, :, j * P : (j + 1) * P, :])
         kernel_codes = keep.tile([P, PASSES * D], U32, align_bytes=64)
         kernel_scales = keep.tile([P, PASSES * D], U8, align_bytes=64)
+
+        grouped_of = {}
+
+        def front(t):
+            g_tile = g_loaded[t // TILES_PER_LOAD][:, t % TILES_PER_LOAD, :]
+            z_tile = z_loaded[t // TILES_PER_LOAD][:, t % TILES_PER_LOAD, :]
+            masked = work.tile([P, L], BF16)
+            nc.vector.scalar_tensor_tensor(
+                out=masked[:], in0=z_tile, scalar=0.0, in1=g_tile, op0=ALU.is_gt, op1=ALU.mult
+            )
+            dz = work.tile([P, L], BF16)
+            nc.vector.tensor_scalar(
+                out=dz[:], in0=masked[:], scalar1=inv_factor[:, t : t + 1], scalar2=None, op0=ALU.mult
+            )
+            grouped = work.tile([P, PASSES * P * PACK], BF16, align_bytes=64)
+            turn_rows(
+                nc,
+                banks,
+                identity[:],
+                dz[:],
+                grouped[:].bitcast(F32).rearrange("p (g r u) -> p g r u", g=PASSES, u=HALVES),
+            )
+            grouped_of[t] = grouped
+
+        def back(t):
+            dz_codes = work.tile([P, PASSES * P], U32, align_bytes=64)
+            dz_scales = work.tile([P, PASSES * P], U8, align_bytes=64)
+            nc.vector.quantize_mx(
+                out=dz_codes[:].bitcast(E5M2_X4), scales=dz_scales[:], in_=grouped_of[t][:]
+            )
+            acc = sums.tile([P, D], F32)
+            for g in range(PASSES):
+                nodes = slice(g * P, (g + 1) * P)
+                columns = slice(g * D, (g + 1) * D)
+                nc.tensor.matmul_mx(
+                    out=acc[:],
+                    lhsT=dz_codes[:, nodes].bitcast(E5M2_X4),
+                    lhsT_scale=dz_scales[:, nodes],
+                    rhs=kernel_codes[:, columns].bitcast(E4M3_X4),
+                    rhs_scale=kernel_scales[:, columns],
+                    start=(g == 0),
+                    stop=(g == PASSES - 1),
+                )
+            s = t // TILES_PER_STORE
+            nc.scalar.copy(out=out_stored[s][:, t % TILES_PER_STORE, :], in_=acc[:])
+            if t % TILES_PER_STORE == TILES_PER_STORE - 1:
+                tiles = slice(s * TILES_PER_STORE, (s + 1) * TILES_PER_STORE)
+                nc.sync.dma_start(out=out_rows[:, tiles, :], in_=out_stored[s][:])
+
+        for t in range(LAG):
+            front(t)
         nc.vector.quantize_mx(
             out=kernel_codes[:].bitcast(E4M3_X4), scales=kernel_scales[:], in_=kernel_grouped[:]
         )
-
-        dz_codes = keep.tile([P, ROW_TILES, PASSES * P], U32, align_bytes=64)
-        dz_scales = keep.tile([P, ROW_TILES, PASSES * P], U8, align_bytes=64)
-        for s in range(STORES):
-            out_sb = results.tile([P, TILES_PER_STORE, D], F32)
-            for i in range(TILES_PER_STORE):
-                t = s * TILES_PER_STORE + i
-                g_tile = g_loaded[t // TILES_PER_LOAD][:, t % TILES_PER_LOAD, :]
-                z_tile = z_loaded[t // TILES_PER_LOAD][:, t % TILES_PER_LOAD, :]
-
-                masked = work.tile([P, L], BF16)
-                nc.vector.scalar_tensor_tensor(
-                    out=masked[:], in0=z_tile, scalar=0.0, in1=g_tile, op0=ALU.is_gt, op1=ALU.mult
-                )
-                dz = work.tile([P, L], BF16)
-                nc.vector.tensor_scalar(
-                    out=dz[:], in0=masked[:], scalar1=inv_factor[:, t : t + 1], scalar2=None, op0=ALU.mult
-                )
-
-                grouped = work.tile([P, PASSES * P * PACK], BF16, align_bytes=64)
-                turn_rows(
-                    nc,
-                    banks,
-                    identity[:],
-                    dz[:],
-                    grouped[:].bitcast(F32).rearrange("p (g r u) -> p g r u", g=PASSES, u=HALVES),
-                )
-                nc.vector.quantize_mx(
-                    out=dz_codes[:, t, :].bitcast(E5M2_X4), scales=dz_scales[:, t, :], in_=grouped[:]
-                )
-
-                acc = sums.tile([P, D], F32)
-                for g in range(PASSES):
-                    nodes = slice(g * P, (g + 1) * P)
-                    columns = slice(g * D, (g + 1) * D)
-                    nc.tensor.matmul_mx(
-                        out=acc[:],
-                        lhsT=dz_codes[:, t, nodes].bitcast(E5M2_X4),
-                        lhsT_scale=dz_scales[:, t, nodes],
-                        rhs=kernel_codes[:, columns].bitcast(E4M3_X4),
-                        rhs_scale=kernel_scales[:, columns],
-                        start=(g == 0),
-                        stop=(g == PASSES - 1),
-                    )
-                nc.scalar.copy(out=out_sb[:, i, :], in_=acc[:])
-            tiles = slice(s * TILES_PER_STORE, (s + 1) * TILES_PER_STORE)
-            nc.sync.dma_start(out=out_rows[:, tiles, :], in_=out_sb[:])
+        for t in range(LAG, ROW_TILES):
+            front(t)
+            back(t - LAG)
+        for t in range(ROW_TILES - LAG, ROW_TILES):
+            back(t)

@@ -100,18 +100,23 @@ def tile_singlegcnlayer_t_v_kernel(tc, targets, neighbors, a, kernel, z, grad_ou
         kernel_codes = keep.tile([P, PASSES * D], U32, align_bytes=64)
         kernel_scales = keep.tile([P, PASSES * D], U8, align_bytes=64)
 
+        masked_of = {}
         grouped_of = {}
+        codes_of = {}
 
-        def front(t):
+        def mask(t):
             g_tile = g_loaded[t // TILES_PER_LOAD][:, t % TILES_PER_LOAD, :]
             z_tile = z_loaded[t // TILES_PER_LOAD][:, t % TILES_PER_LOAD, :]
             masked = work.tile([P, L], BF16)
             nc.vector.scalar_tensor_tensor(
                 out=masked[:], in0=z_tile, scalar=0.0, in1=g_tile, op0=ALU.is_gt, op1=ALU.mult
             )
+            masked_of[t] = masked
+
+        def scale_and_turn(t):
             dz = work.tile([P, L], BF16)
             nc.vector.tensor_scalar(
-                out=dz[:], in0=masked[:], scalar1=inv_factor[:, t : t + 1], scalar2=None, op0=ALU.mult
+                out=dz[:], in0=masked_of[t][:], scalar1=inv_factor[:, t : t + 1], scalar2=None, op0=ALU.mult
             )
             grouped = work.tile([P, PASSES * P * PACK], BF16, align_bytes=64)
             turn_rows(
@@ -123,12 +128,16 @@ def tile_singlegcnlayer_t_v_kernel(tc, targets, neighbors, a, kernel, z, grad_ou
             )
             grouped_of[t] = grouped
 
-        def back(t):
+        def quantise(t):
             dz_codes = work.tile([P, PASSES * P], U32, align_bytes=64)
             dz_scales = work.tile([P, PASSES * P], U8, align_bytes=64)
             nc.vector.quantize_mx(
                 out=dz_codes[:].bitcast(E5M2_X4), scales=dz_scales[:], in_=grouped_of[t][:]
             )
+            codes_of[t] = (dz_codes, dz_scales)
+
+        def multiply_and_store(t):
+            dz_codes, dz_scales = codes_of[t]
             acc = sums.tile([P, D], F32)
             for g in range(PASSES):
                 nodes = slice(g * P, (g + 1) * P)
@@ -148,13 +157,16 @@ def tile_singlegcnlayer_t_v_kernel(tc, targets, neighbors, a, kernel, z, grad_ou
                 tiles = slice(s * TILES_PER_STORE, (s + 1) * TILES_PER_STORE)
                 nc.sync.dma_start(out=out_rows[:, tiles, :], in_=out_stored[s][:])
 
-        for t in range(LAG):
-            front(t)
-        nc.vector.quantize_mx(
-            out=kernel_codes[:].bitcast(E4M3_X4), scales=kernel_scales[:], in_=kernel_grouped[:]
-        )
-        for t in range(LAG, ROW_TILES):
-            front(t)
-            back(t - LAG)
-        for t in range(ROW_TILES - LAG, ROW_TILES):
-            back(t)
+        for step in range(ROW_TILES + LAG):
+            if step == LAG:
+                nc.vector.quantize_mx(
+                    out=kernel_codes[:].bitcast(E4M3_X4), scales=kernel_scales[:], in_=kernel_grouped[:]
+                )
+            if step < ROW_TILES:
+                mask(step)
+            if step >= LAG:
+                quantise(step - LAG)
+            if step < ROW_TILES:
+                scale_and_turn(step)
+            if step >= LAG:
+                multiply_and_store(step - LAG)

@@ -24,10 +24,10 @@ D = 512
 PASSES = L // (P * PACK)
 ROW_TILES = NODES // P
 KERNEL_TILES = D // P
-TILES_PER_LOAD = 1
-TILES_PER_STORE = 2
-LOADS = ROW_TILES // TILES_PER_LOAD
-STORES = ROW_TILES // TILES_PER_STORE
+LOAD_TILES = [1, 1] + [2] * ((ROW_TILES - 2) // 2)
+STORE_TILES = LOAD_TILES[::-1]
+LOADS = len(LOAD_TILES)
+STORES = len(STORE_TILES)
 LAG = 2
 
 FLOPS = 2 * NODES * L * D
@@ -64,20 +64,25 @@ def tile_singlegcnlayer_t_v_kernel(tc, targets, neighbors, a, kernel, z, grad_ou
         nc.sync.dma_start(out=a_sb[:], in_=a_rows)
         kernel_sb = keep.tile([P, KERNEL_TILES, L], BF16)
         nc.sync.dma_start(out=kernel_sb[:], in_=kernel_rows)
-        g_loaded = []
-        z_loaded = []
-        for c in range(LOADS):
-            tiles = slice(c * TILES_PER_LOAD, (c + 1) * TILES_PER_LOAD)
-            g_sb = stream.tile([P, TILES_PER_LOAD, L], BF16)
+        g_of = []
+        z_of = []
+        for count in LOAD_TILES:
+            tiles = slice(len(g_of), len(g_of) + count)
+            g_sb = stream.tile([P, count, L], BF16)
             nc.sync.dma_start(out=g_sb[:], in_=g_rows[:, tiles, :])
-            g_loaded.append(g_sb)
-            z_sb = stream.tile([P, TILES_PER_LOAD, L], F32)
+            z_sb = stream.tile([P, count, L], F32)
             nc.sync.dma_start(out=z_sb[:], in_=z_rows[:, tiles, :])
-            z_loaded.append(z_sb)
-        out_stored = []
-        for s in range(STORES):
-            out_sb = results.tile([P, TILES_PER_STORE, D], F32)
-            out_stored.append(out_sb)
+            for i in range(count):
+                g_of.append(g_sb[:, i, :])
+                z_of.append(z_sb[:, i, :])
+        out_of = []
+        store_after = {}
+        for count in STORE_TILES:
+            tiles = slice(len(out_of), len(out_of) + count)
+            out_sb = results.tile([P, count, D], F32)
+            for i in range(count):
+                out_of.append(out_sb[:, i, :])
+            store_after[len(out_of) - 1] = (out_rows[:, tiles, :], out_sb)
 
         identity = keep.tile([P, P], F32)
         make_identity(nc, identity[:])
@@ -105,11 +110,9 @@ def tile_singlegcnlayer_t_v_kernel(tc, targets, neighbors, a, kernel, z, grad_ou
         codes_of = {}
 
         def mask(t):
-            g_tile = g_loaded[t // TILES_PER_LOAD][:, t % TILES_PER_LOAD, :]
-            z_tile = z_loaded[t // TILES_PER_LOAD][:, t % TILES_PER_LOAD, :]
             masked = work.tile([P, L], BF16)
             nc.vector.scalar_tensor_tensor(
-                out=masked[:], in0=z_tile, scalar=0.0, in1=g_tile, op0=ALU.is_gt, op1=ALU.mult
+                out=masked[:], in0=z_of[t], scalar=0.0, in1=g_of[t], op0=ALU.is_gt, op1=ALU.mult
             )
             masked_of[t] = masked
 
@@ -151,11 +154,10 @@ def tile_singlegcnlayer_t_v_kernel(tc, targets, neighbors, a, kernel, z, grad_ou
                     start=(g == 0),
                     stop=(g == PASSES - 1),
                 )
-            s = t // TILES_PER_STORE
-            nc.scalar.copy(out=out_stored[s][:, t % TILES_PER_STORE, :], in_=acc[:])
-            if t % TILES_PER_STORE == TILES_PER_STORE - 1:
-                tiles = slice(s * TILES_PER_STORE, (s + 1) * TILES_PER_STORE)
-                nc.sync.dma_start(out=out_rows[:, tiles, :], in_=out_stored[s][:])
+            nc.scalar.copy(out=out_of[t], in_=acc[:])
+            if t in store_after:
+                rows, out_sb = store_after[t]
+                nc.sync.dma_start(out=rows, in_=out_sb[:])
 
         for step in range(ROW_TILES + LAG):
             if step == LAG:

@@ -29,6 +29,8 @@ STORE_TILES = LOAD_TILES[::-1]
 LOADS = len(LOAD_TILES)
 STORES = len(STORE_TILES)
 LAG = 2
+LEAD = 3
+PRESCALED = list(range(LEAD, ROW_TILES, 3))
 
 FLOPS = 2 * NODES * L * D
 BYTES = NODES * NEIGHBOURS * 2 + D * L * 2 + NODES * L * 4 + NODES * L * 2 + NODES * D * 4
@@ -106,6 +108,7 @@ def tile_singlegcnlayer_t_v_kernel(tc, targets, neighbors, a, kernel, z, grad_ou
         kernel_scales = keep.tile([P, PASSES * D], U8, align_bytes=64)
 
         masked_of = {}
+        scaled_of = {}
         grouped_of = {}
         codes_of = {}
 
@@ -116,11 +119,23 @@ def tile_singlegcnlayer_t_v_kernel(tc, targets, neighbors, a, kernel, z, grad_ou
             )
             masked_of[t] = masked
 
+        def prescale(t):
+            scaled = work.tile([P, L], F32)
+            nc.scalar.activation(
+                out=scaled[:], in_=g_of[t], func=mybir.ActivationFunctionType.Copy, scale=inv_factor[:, t : t + 1]
+            )
+            scaled_of[t] = scaled
+
         def scale_and_turn(t):
             dz = work.tile([P, L], BF16)
-            nc.vector.tensor_scalar(
-                out=dz[:], in0=masked_of[t][:], scalar1=inv_factor[:, t : t + 1], scalar2=None, op0=ALU.mult
-            )
+            if t in PRESCALED:
+                nc.vector.scalar_tensor_tensor(
+                    out=dz[:], in0=z_of[t], scalar=0.0, in1=scaled_of[t][:], op0=ALU.is_gt, op1=ALU.mult
+                )
+            else:
+                nc.vector.tensor_scalar(
+                    out=dz[:], in0=masked_of[t][:], scalar1=inv_factor[:, t : t + 1], scalar2=None, op0=ALU.mult
+                )
             grouped = work.tile([P, PASSES * P * PACK], BF16, align_bytes=64)
             turn_rows(
                 nc,
@@ -164,11 +179,15 @@ def tile_singlegcnlayer_t_v_kernel(tc, targets, neighbors, a, kernel, z, grad_ou
                 nc.vector.quantize_mx(
                     out=kernel_codes[:].bitcast(E4M3_X4), scales=kernel_scales[:], in_=kernel_grouped[:]
                 )
-            if step < ROW_TILES:
+            if step < ROW_TILES and step not in PRESCALED:
                 mask(step)
-            if step >= LAG:
+            if step >= LAG and step not in PRESCALED:
                 quantise(step - LAG)
             if step < ROW_TILES:
                 scale_and_turn(step)
+            if step >= LAG and step in PRESCALED:
+                quantise(step - LAG)
             if step >= LAG:
                 multiply_and_store(step - LAG)
+            if step + LEAD in PRESCALED:
+                prescale(step + LEAD)

@@ -25,7 +25,7 @@ PASSES = L // (P * PACK)
 ROW_TILES = NODES // P
 KERNEL_TILES = D // P
 LOAD_TILES = [1, 1] + [2] * ((ROW_TILES - 2) // 2)
-STORE_TILES = LOAD_TILES[::-1]
+STORE_TILES = [2] * (ROW_TILES // 4) + [1] * (ROW_TILES // 2)
 LOADS = len(LOAD_TILES)
 STORES = len(STORE_TILES)
 LAG = 2
@@ -107,17 +107,16 @@ def tile_singlegcnlayer_t_v_kernel(tc, targets, neighbors, a, kernel, z, grad_ou
         kernel_codes = keep.tile([P, PASSES * D], U32, align_bytes=64)
         kernel_scales = keep.tile([P, PASSES * D], U8, align_bytes=64)
 
-        masked_of = {}
         scaled_of = {}
         grouped_of = {}
         codes_of = {}
 
-        def mask(t):
-            masked = work.tile([P, L], BF16)
-            nc.vector.scalar_tensor_tensor(
-                out=masked[:], in0=z_of[t], scalar=0.0, in1=g_of[t], op0=ALU.is_gt, op1=ALU.mult
+        def scale(t):
+            scaled = work.tile([P, L], BF16, name="rounded")
+            nc.vector.tensor_scalar(
+                out=scaled[:], in0=g_of[t], scalar1=inv_factor[:, t : t + 1], scalar2=None, op0=ALU.mult
             )
-            masked_of[t] = masked
+            scaled_of[t] = scaled
 
         def prescale(t):
             scaled = work.tile([P, L], F32)
@@ -126,16 +125,11 @@ def tile_singlegcnlayer_t_v_kernel(tc, targets, neighbors, a, kernel, z, grad_ou
             )
             scaled_of[t] = scaled
 
-        def scale_and_turn(t):
+        def mask_and_turn(t):
             dz = work.tile([P, L], BF16)
-            if t in PRESCALED:
-                nc.vector.scalar_tensor_tensor(
-                    out=dz[:], in0=z_of[t], scalar=0.0, in1=scaled_of[t][:], op0=ALU.is_gt, op1=ALU.mult
-                )
-            else:
-                nc.vector.tensor_scalar(
-                    out=dz[:], in0=masked_of[t][:], scalar1=inv_factor[:, t : t + 1], scalar2=None, op0=ALU.mult
-                )
+            nc.vector.scalar_tensor_tensor(
+                out=dz[:], in0=z_of[t], scalar=0.0, in1=scaled_of[t][:], op0=ALU.is_gt, op1=ALU.mult
+            )
             grouped = work.tile([P, PASSES * P * PACK], BF16, align_bytes=64)
             turn_rows(
                 nc,
@@ -174,20 +168,18 @@ def tile_singlegcnlayer_t_v_kernel(tc, targets, neighbors, a, kernel, z, grad_ou
                 rows, out_sb = store_after[t]
                 nc.sync.dma_start(out=rows, in_=out_sb[:])
 
+        scale(0)
         for step in range(ROW_TILES + LAG):
             if step == LAG:
                 nc.vector.quantize_mx(
                     out=kernel_codes[:].bitcast(E4M3_X4), scales=kernel_scales[:], in_=kernel_grouped[:]
                 )
-            if step < ROW_TILES and step not in PRESCALED:
-                mask(step)
-            if step >= LAG and step not in PRESCALED:
-                quantise(step - LAG)
             if step < ROW_TILES:
-                scale_and_turn(step)
-            if step >= LAG and step in PRESCALED:
-                quantise(step - LAG)
+                mask_and_turn(step)
+            if step + 1 < ROW_TILES and step + 1 not in PRESCALED:
+                scale(step + 1)
             if step >= LAG:
+                quantise(step - LAG)
                 multiply_and_store(step - LAG)
             if step + LEAD in PRESCALED:
                 prescale(step + LEAD)

@@ -30,7 +30,7 @@ LOADS = len(LOAD_TILES)
 STORES = len(STORE_TILES)
 LAG = 2
 LEAD = 3
-PRESCALED = list(range(LEAD, ROW_TILES, 3))
+PRESCALED = list(range(LEAD, ROW_TILES, 4))
 
 FLOPS = 2 * NODES * L * D
 BYTES = NODES * NEIGHBOURS * 2 + D * L * 2 + NODES * L * 4 + NODES * L * 2 + NODES * D * 4

from contextlib import ExitStack

import concourse.mybir as mybir
from concourse.masks import make_identity

F32 = mybir.dt.float32
BF16 = mybir.dt.bfloat16
U32 = mybir.dt.uint32
U8 = mybir.dt.uint8
E4M3_X4 = mybir.dt.float8_e4m3fn_x4
E5M2_X4 = mybir.dt.float8_e5m2_x4
ALU = mybir.AluOpType

P = 128
PACK = 4
PAIR = 2
HALVES = PACK // PAIR

NODES = 2 * 1024
NEIGHBOURS = 8
L = 1024
D = 512

PASSES = L // (P * PACK)
ROW_TILES = NODES // P
KERNEL_TILES = D // P
LOAD_TILES = [1, 1] + [2] * ((ROW_TILES - 2) // 2)
STORE_TILES = [2] * (ROW_TILES // 4) + [1] * (ROW_TILES // 2)
LOADS = len(LOAD_TILES)
STORES = len(STORE_TILES)
LAG = 2
LEAD = 3
PRESCALED = list(range(LEAD, ROW_TILES, 4))

FLOPS = 2 * NODES * L * D
BYTES = NODES * NEIGHBOURS * 2 + D * L * 2 + NODES * L * 4 + NODES * L * 2 + NODES * D * 4


def turn_rows(nc, banks, identity, rows, grouped):
    words = rows.bitcast(F32)
    turned = banks.tile([P, PASSES * HALVES, P], F32)
    for i in range(PASSES * HALVES):
        nc.tensor.transpose(turned[:, i, :], words[:, i * P : (i + 1) * P], identity)
    nc.scalar.copy(out=grouped, in_=turned[:].rearrange("p (g u) r -> p g r u", u=HALVES))


def tile_singlegcnlayer_t_v_kernel(tc, targets, neighbors, a, kernel, z, grad_out, out):
    nc = tc.nc

    a_rows = a.flatten_outer_dims().rearrange("(p t) k -> p t k", t=ROW_TILES)
    z_rows = z.flatten_outer_dims().rearrange("(p t) l -> p t l", t=ROW_TILES)
    g_rows = grad_out.flatten_outer_dims().rearrange("(p t) l -> p t l", t=ROW_TILES)
    out_rows = out.flatten_outer_dims().rearrange("(p t) d -> p t d", t=ROW_TILES)
    kernel_rows = kernel.rearrange("(j p) l -> p j l", p=P)

    with ExitStack() as ctx:
        ctx.enter_context(tc.manual_schedule())
        keep = ctx.enter_context(tc.tile_pool(name="keep", bufs=1))
        stream = ctx.enter_context(tc.tile_pool(name="stream", bufs=LOADS))
        results = ctx.enter_context(tc.tile_pool(name="results", bufs=STORES))
        work = ctx.enter_context(tc.tile_pool(name="work", bufs=LAG + 2))
        banks = ctx.enter_context(tc.psum_pool(name="banks", bufs=4))
        sums = ctx.enter_context(tc.psum_pool(name="sums", bufs=4))

        a_sb = keep.tile([P, ROW_TILES, NEIGHBOURS], BF16)
        nc.sync.dma_start(out=a_sb[:], in_=a_rows)
        kernel_sb = keep.tile([P, KERNEL_TILES, L], BF16)
        nc.sync.dma_start(out=kernel_sb[:], in_=kernel_rows)
        g_of = []
        z_of = []
        for count in LOAD_TILES:
            tiles = slice(len(g_of), len(g_of) + count)
            g_sb = stream.tile([P, count, L], BF16)
            nc.sync.dma_start(out=g_sb[:], in_=g_rows[:, tiles, :])
            z_sb = stream.tile([P, count, L], F32)
            nc.sync.dma_start(out=z_sb[:], in_=z_rows[:, tiles, :])
            for i in range(count):
                g_of.append(g_sb[:, i, :])
                z_of.append(z_sb[:, i, :])
        out_of = []
        store_after = {}
        for count in STORE_TILES:
            tiles = slice(len(out_of), len(out_of) + count)
            out_sb = results.tile([P, count, D], F32)
            for i in range(count):
                out_of.append(out_sb[:, i, :])
            store_after[len(out_of) - 1] = (out_rows[:, tiles, :], out_sb)

        identity = keep.tile([P, P], F32)
        make_identity(nc, identity[:])

        degree = keep.tile([P, ROW_TILES], F32)
        nc.vector.tensor_reduce(out=degree[:], in_=a_sb[:], axis=mybir.AxisListType.X, op=ALU.add)
        factor = keep.tile([P, ROW_TILES], F32)
        nc.vector.scalar_tensor_tensor(
            out=factor[:], in0=degree[:], scalar=0.5, in1=degree[:], op0=ALU.is_le, op1=ALU.max
        )
        inv_factor = keep.tile([P, ROW_TILES], F32)
        nc.vector.reciprocal(out=inv_factor[:], in_=factor[:])

        kernel_grouped = keep.tile([P, PASSES * D * PACK], BF16, align_bytes=64)
        kernel_words = kernel_grouped[:].bitcast(F32).rearrange(
            "p (g d u) -> p g d u", g=PASSES, u=HALVES
        )
        for j in range(KERNEL_TILES):
            turn_rows(nc, banks, identity[:], kernel_sb[:, j, :], kernel_words[:, :, j * P : (j + 1) * P, :])
        kernel_codes = keep.tile([P, PASSES * D], U32, align_bytes=64)
        kernel_scales = keep.tile([P, PASSES * D], U8, align_bytes=64)

        scaled_of = {}
        grouped_of = {}
        codes_of = {}

        def scale(t):
            scaled = work.tile([P, L], BF16, name="rounded")
            nc.vector.tensor_scalar(
                out=scaled[:], in0=g_of[t], scalar1=inv_factor[:, t : t + 1], scalar2=None, op0=ALU.mult
            )
            scaled_of[t] = scaled

        def prescale(t):
            scaled = work.tile([P, L], F32)
            nc.scalar.activation(
                out=scaled[:], in_=g_of[t], func=mybir.ActivationFunctionType.Copy, scale=inv_factor[:, t : t + 1]
            )
            scaled_of[t] = scaled

        def mask_and_turn(t):
            dz = work.tile([P, L], BF16)
            nc.vector.scalar_tensor_tensor(
                out=dz[:], in0=z_of[t], scalar=0.0, in1=scaled_of[t][:], op0=ALU.is_gt, op1=ALU.mult
            )
            grouped = work.tile([P, PASSES * P * PACK], BF16, align_bytes=64)
            turn_rows(
                nc,
                banks,
                identity[:],
                dz[:],
                grouped[:].bitcast(F32).rearrange("p (g r u) -> p g r u", g=PASSES, u=HALVES),
            )
            grouped_of[t] = grouped

        def quantise(t):
            dz_codes = work.tile([P, PASSES * P], U32, align_bytes=64)
            dz_scales = work.tile([P, PASSES * P], U8, align_bytes=64)
            nc.vector.quantize_mx(
                out=dz_codes[:].bitcast(E5M2_X4), scales=dz_scales[:], in_=grouped_of[t][:]
            )
            codes_of[t] = (dz_codes, dz_scales)

        def multiply_and_store(t):
            dz_codes, dz_scales = codes_of[t]
            acc = sums.tile([P, D], F32)
            for g in range(PASSES):
                nodes = slice(g * P, (g + 1) * P)
                columns = slice(g * D, (g + 1) * D)
                nc.tensor.matmul_mx(
                    out=acc[:],
                    lhsT=dz_codes[:, nodes].bitcast(E5M2_X4),
                    lhsT_scale=dz_scales[:, nodes],
                    rhs=kernel_codes[:, columns].bitcast(E4M3_X4),
                    rhs_scale=kernel_scales[:, columns],
                    start=(g == 0),
                    stop=(g == PASSES - 1),
                )
            nc.scalar.copy(out=out_of[t], in_=acc[:])
            if t in store_after:
                rows, out_sb = store_after[t]
                nc.sync.dma_start(out=rows, in_=out_sb[:])

        scale(0)
        for step in range(ROW_TILES + LAG):
            if step == LAG:
                nc.vector.quantize_mx(
                    out=kernel_codes[:].bitcast(E4M3_X4), scales=kernel_scales[:], in_=kernel_grouped[:]
                )
            if step < ROW_TILES:
                mask_and_turn(step)
            if step + 1 < ROW_TILES and step + 1 not in PRESCALED:
                scale(step + 1)
            if step >= LAG:
                quantise(step - LAG)
                multiply_and_store(step - LAG)
            if step + LEAD in PRESCALED:
                prescale(step + LEAD)
